import numpy as np
import ml_dtypes

BF16 = ml_dtypes.bfloat16


def bf(x):
    return np.asarray(x, np.float32).astype(BF16)


def f32(x):
    return np.asarray(x, np.float32)


def f64(x):
    return np.asarray(x).astype(np.float64)


def striped(idx):
    return np.tile(idx.reshape(-1, 16).T, (8, 1))


F, S, T, TN, M, R, H, N = 128, 1024, 16, 8, 128, 8, 512, 4096


def setup_inputs():
    return {"table": bf(np.random.standard_normal((F, S))), "templates": bf(np.random.uniform(size=(F, M))), "offs": striped(np.concatenate([np.random.permutation(S)[:H] for _ in range(R)]))}


def reference(table, templates, offs):
    idx = offs[:16].T.reshape(-1)
    xg = f64(table)[:, idx]
    w = f64(templates)
    return (np.sum(xg * xg, axis=0)[None, :] + np.sum(w * w, axis=0)[:, None] - 2.0 * (w.T @ xg)) / F

@@ -1,0 +1,68 @@
+import concourse.mybir as mybir
+from concourse.masks import make_identity
+
+BF16, F32, U16 = mybir.dt.bfloat16, mybir.dt.float32, mybir.dt.uint16
+MULT, ADD = mybir.AluOpType.mult, mybir.AluOpType.add
+IDENTITY = mybir.ActivationFunctionType.Identity
+
+F = 128
+S = 1024
+M = 128
+N = 4096
+PIECE = 512
+N_PIECES = N // PIECE
+PIECE_COLS = PIECE // 16
+TABLE_LOADS = 4
+HALF = PIECE // 2
+
+FLOPS = 2 * F * M * N + 2 * F * N + 2 * F * M + 3 * M * N
+
+
+def tile_ot_gnn_layer_kernel(tc, table, templates, offs, out):
+    nc = tc.nc
+    with (
+        tc.tile_pool(name="held", bufs=1) as held,
+        tc.tile_pool(name="staging", bufs=N_PIECES) as staging,
+        tc.psum_pool(name="norm_bank", bufs=1) as norm_bank,
+        tc.psum_pool(name="banks", bufs=4) as banks,
+    ):
+        temps = held.tile([F, M], BF16, name="temps")
+        nc.sync.dma_start(temps[:], templates)
+        offsets = held.tile([128, N // 16], U16, name="offsets")
+        nc.sync.dma_start(offsets[:], offs)
+        nodes = held.tile([F, S], BF16, name="nodes")
+        for b in range(TABLE_LOADS):
+            cols = slice(b * (S // TABLE_LOADS), (b + 1) * (S // TABLE_LOADS))
+            queue = nc.scalar if b % 2 == 0 else nc.sync
+            queue.dma_start(nodes[:, cols], table[:, cols])
+
+        minus_half = held.tile([F, M], BF16, name="minus_half")
+        nc.vector.memset(minus_half[:], -0.5)
+        identity = held.tile([M, M], F32, name="identity")
+        make_identity(nc, identity[:])
+
+        gram = norm_bank.tile([M, M], F32, name="gram")
+        nc.tensor.matmul(gram[:], temps[:], temps[:], start=True, stop=True)
+
+        nodes_sq = held.tile([F, S], BF16, name="nodes_sq")
+        nc.vector.tensor_tensor(nodes_sq[:], nodes[:], nodes[:], MULT)
+
+        diagonal = held.tile([M, M], F32, name="diagonal")
+        temp_norm = held.tile([M, 1], F32, name="temp_norm")
+        nc.vector.scalar_tensor_tensor(diagonal[:], gram[:], 1.0 / F, identity[:], MULT, MULT, accum_out=temp_norm[:])
+
+        for k in range(N_PIECES):
+            piece = offsets[:, k * PIECE_COLS : (k + 1) * PIECE_COLS]
+            bank = banks.tile([M, PIECE], F32, name="bank")
+            nc.tensor.matmul(bank[:], temps[:], nodes[:].indirect(piece), start=True, stop=False)
+            nc.tensor.matmul(bank[:], minus_half[:], nodes_sq[:].indirect(piece), start=False, stop=True)
+
+            cost = staging.tile([M, PIECE], F32, name="cost")
+            for h in range(2):
+                cols = slice(h * HALF, (h + 1) * HALF)
+                if k % 2 == 0:
+                    nc.scalar.activation(cost[:, cols], bank[:, cols], IDENTITY, bias=temp_norm[:], scale=-2.0 / F)
+                else:
+                    nc.vector.tensor_scalar(cost[:, cols], bank[:, cols], -2.0 / F, temp_norm[:], MULT, ADD)
+                first = k * PIECE + h * HALF
+                nc.sync.dma_start(out[:, first : first + HALF], cost[:, cols])

@@ -3,7 +3,6 @@ from concourse.masks import make_identity
 
 BF16, F32, U16 = mybir.dt.bfloat16, mybir.dt.float32, mybir.dt.uint16
 MULT, ADD = mybir.AluOpType.mult, mybir.AluOpType.add
-IDENTITY = mybir.ActivationFunctionType.Identity
 
 F = 128
 S = 1024
@@ -60,9 +59,6 @@ def tile_ot_gnn_layer_kernel(tc, table, templates, offs, out):
             cost = staging.tile([M, PIECE], F32, name="cost")
             for h in range(2):
                 cols = slice(h * HALF, (h + 1) * HALF)
-                if k % 2 == 0:
-                    nc.scalar.activation(cost[:, cols], bank[:, cols], IDENTITY, bias=temp_norm[:], scale=-2.0 / F)
-                else:
-                    nc.vector.tensor_scalar(cost[:, cols], bank[:, cols], -2.0 / F, temp_norm[:], MULT, ADD)
+                nc.vector.tensor_scalar(cost[:, cols], bank[:, cols], -2.0 / F, temp_norm[:], MULT, ADD)
                 first = k * PIECE + h * HALF
                 nc.sync.dma_start(out[:, first : first + HALF], cost[:, cols])

@@ -12,6 +12,7 @@ PIECE = 512
 N_PIECES = N // PIECE
 PIECE_COLS = PIECE // 16
 TABLE_LOADS = 4
+OPENED = 1
 HALF = PIECE // 2
 
 FLOPS = 2 * F * M * N + 2 * F * N + 2 * F * M + 3 * M * N
@@ -35,13 +36,21 @@ def tile_ot_gnn_layer_kernel(tc, table, templates, offs, out):
             queue = nc.scalar if b % 2 == 0 else nc.sync
             queue.dma_start(nodes[:, cols], table[:, cols])
 
-        minus_half = held.tile([F, M], BF16, name="minus_half")
+        minus_half = held.tile([F, PIECE], BF16, name="minus_half")
         nc.vector.memset(minus_half[:], -0.5)
         identity = held.tile([M, M], F32, name="identity")
         make_identity(nc, identity[:])
 
         gram = norm_bank.tile([M, M], F32, name="gram")
         nc.tensor.matmul(gram[:], temps[:], temps[:], start=True, stop=True)
+
+        temps_sq = held.tile([F, M], BF16, name="temps_sq")
+        nc.vector.tensor_tensor(temps_sq[:], temps[:], temps[:], MULT)
+        opened = []
+        for k in range(OPENED):
+            bank = banks.tile([M, PIECE], F32, name="bank")
+            nc.tensor.matmul(bank[:], temps_sq[:], minus_half[:], start=True, stop=False)
+            opened.append(bank)
 
         nodes_sq = held.tile([F, S], BF16, name="nodes_sq")
         nc.vector.tensor_tensor(nodes_sq[:], nodes[:], nodes[:], MULT)
@@ -52,13 +61,16 @@ def tile_ot_gnn_layer_kernel(tc, table, templates, offs, out):
 
         for k in range(N_PIECES):
             piece = offsets[:, k * PIECE_COLS : (k + 1) * PIECE_COLS]
-            bank = banks.tile([M, PIECE], F32, name="bank")
-            nc.tensor.matmul(bank[:], temps[:], nodes[:].indirect(piece), start=True, stop=False)
-            nc.tensor.matmul(bank[:], minus_half[:], nodes_sq[:].indirect(piece), start=False, stop=True)
+            bank = opened[k] if k < OPENED else banks.tile([M, PIECE], F32, name="bank")
+            nc.tensor.matmul(bank[:], temps[:], nodes[:].indirect(piece), start=k >= OPENED, stop=False)
+            nc.tensor.matmul(bank[:], minus_half[:, :M], nodes_sq[:].indirect(piece), start=False, stop=True)
 
             cost = staging.tile([M, PIECE], F32, name="cost")
             for h in range(2):
                 cols = slice(h * HALF, (h + 1) * HALF)
-                nc.vector.tensor_scalar(cost[:, cols], bank[:, cols], -2.0 / F, temp_norm[:], MULT, ADD)
+                if k < OPENED:
+                    nc.vector.tensor_scalar_mul(cost[:, cols], bank[:, cols], -2.0 / F)
+                else:
+                    nc.vector.tensor_scalar(cost[:, cols], bank[:, cols], -2.0 / F, temp_norm[:], MULT, ADD)
                 first = k * PIECE + h * HALF
                 nc.sync.dma_start(out[:, first : first + HALF], cost[:, cols])

import concourse.mybir as mybir
from concourse.masks import make_identity

BF16, F32, U16 = mybir.dt.bfloat16, mybir.dt.float32, mybir.dt.uint16
MULT, ADD = mybir.AluOpType.mult, mybir.AluOpType.add

F = 128
S = 1024
M = 128
N = 4096
PIECE = 512
N_PIECES = N // PIECE
PIECE_COLS = PIECE // 16
TABLE_LOADS = 4
OPENED = 1
HALF = PIECE // 2

FLOPS = 2 * F * M * N + 2 * F * N + 2 * F * M + 3 * M * N


def tile_ot_gnn_layer_kernel(tc, table, templates, offs, out):
    nc = tc.nc
    with (
        tc.tile_pool(name="held", bufs=1) as held,
        tc.tile_pool(name="staging", bufs=N_PIECES) as staging,
        tc.psum_pool(name="norm_bank", bufs=1) as norm_bank,
        tc.psum_pool(name="banks", bufs=4) as banks,
    ):
        temps = held.tile([F, M], BF16, name="temps")
        nc.sync.dma_start(temps[:], templates)
        offsets = held.tile([128, N // 16], U16, name="offsets")
        nc.sync.dma_start(offsets[:], offs)
        nodes = held.tile([F, S], BF16, name="nodes")
        for b in range(TABLE_LOADS):
            cols = slice(b * (S // TABLE_LOADS), (b + 1) * (S // TABLE_LOADS))
            queue = nc.scalar if b % 2 == 0 else nc.sync
            queue.dma_start(nodes[:, cols], table[:, cols])

        minus_half = held.tile([F, PIECE], BF16, name="minus_half")
        nc.vector.memset(minus_half[:], -0.5)
        identity = held.tile([M, M], F32, name="identity")
        make_identity(nc, identity[:])

        gram = norm_bank.tile([M, M], F32, name="gram")
        nc.tensor.matmul(gram[:], temps[:], temps[:], start=True, stop=True)

        temps_sq = held.tile([F, M], BF16, name="temps_sq")
        nc.vector.tensor_tensor(temps_sq[:], temps[:], temps[:], MULT)
        opened = []
        for k in range(OPENED):
            bank = banks.tile([M, PIECE], F32, name="bank")
            nc.tensor.matmul(bank[:], temps_sq[:], minus_half[:], start=True, stop=False)
            opened.append(bank)

        nodes_sq = held.tile([F, S], BF16, name="nodes_sq")
        nc.vector.tensor_tensor(nodes_sq[:], nodes[:], nodes[:], MULT)

        diagonal = held.tile([M, M], F32, name="diagonal")
        temp_norm = held.tile([M, 1], F32, name="temp_norm")
        nc.vector.scalar_tensor_tensor(diagonal[:], gram[:], 1.0 / F, identity[:], MULT, MULT, accum_out=temp_norm[:])

        for k in range(N_PIECES):
            piece = offsets[:, k * PIECE_COLS : (k + 1) * PIECE_COLS]
            bank = opened[k] if k < OPENED else banks.tile([M, PIECE], F32, name="bank")
            nc.tensor.matmul(bank[:], temps[:], nodes[:].indirect(piece), start=k >= OPENED, stop=False)
            nc.tensor.matmul(bank[:], minus_half[:, :M], nodes_sq[:].indirect(piece), start=False, stop=True)

            cost = staging.tile([M, PIECE], F32, name="cost")
            for h in range(2):
                cols = slice(h * HALF, (h + 1) * HALF)
                if k < OPENED:
                    nc.vector.tensor_scalar_mul(cost[:, cols], bank[:, cols], -2.0 / F)
                else:
                    nc.vector.tensor_scalar(cost[:, cols], bank[:, cols], -2.0 / F, temp_norm[:], MULT, ADD)
                first = k * PIECE + h * HALF
                nc.sync.dma_start(out[:, first : first + HALF], cost[:, cols])
